import numpy as np
import ml_dtypes


def mxq(x, axis, fmt="e4m3"):
    dtype, down = {"e4m3": (ml_dtypes.float8_e4m3fn, 7), "e5m2": (ml_dtypes.float8_e5m2, 14)}[fmt]
    v = np.moveaxis(np.asarray(x, np.float32).astype(ml_dtypes.bfloat16).astype(np.float64), axis, -1)
    blocks = v.reshape(v.shape[:-1] + (-1, 32))
    amax = np.abs(blocks).max(-1, keepdims=True)
    byte = np.maximum(np.where(amax > 0, np.frexp(amax)[1] - 1 + 127, 0) - down, 1)
    scale = np.exp2(byte - 127.0)
    codes = (blocks / scale).astype(np.float32).astype(dtype).astype(np.float64)
    return np.moveaxis((codes * scale).reshape(v.shape), -1, axis)


WIDE = False


def mx_kscale(k):
    if not WIDE:
        return np.ones(k)
    levels = np.array([18, -18])
    if k % 512:
        return np.exp2(np.random.permutation(np.resize(levels, k // 32))).repeat(32)
    a = np.empty((k // 512, 16))
    for p in range(k // 512):
        a[p, :8] = np.random.permutation(np.resize(levels, 8))
        for g in range(8):
            far = levels[np.abs(levels - a[p, g]) >= 10]
            a[p, g + 8] = far[np.random.randint(len(far))]
    return np.exp2(a.ravel()).repeat(32)


BF16 = ml_dtypes.bfloat16


def bf(x):
    return np.asarray(x, np.float32).astype(BF16)


def f64(x):
    return np.asarray(x).astype(np.float64)


B, S, DIM, H, NOPE, ROPE = 8, 128, 1536, 8, 128, 64
QK = NOPE + ROPE
T = B * S
J = H * QK


def rope_backward(g, freqs):
    b, s, h, d = g.shape
    gr = g.reshape(b, s, h, d // 2, 2)
    cos = np.cos(freqs)[None, :, None, :]
    sin = np.sin(freqs)[None, :, None, :]
    out = np.stack([gr[..., 0] * cos + gr[..., 1] * sin,
                    gr[..., 1] * cos - gr[..., 0] * sin], axis=-1)
    return out.reshape(b, s, h, d)


def setup_inputs():
    s = mx_kscale(T).reshape(B, S, 1)
    u = mx_kscale(J)
    ug = np.concatenate([u[:H * NOPE].reshape(H, NOPE), u[H * NOPE:].reshape(H, ROPE)], axis=-1)
    inv_freq = 1.0 / (10000.0 ** (np.arange(0, ROPE, 2) / ROPE))
    ang = np.arange(S)[:, None] * inv_freq[None, :]
    ang = np.angle(np.exp(1j * ang))
    x = bf(np.random.standard_normal((B, S, DIM)) * s)
    w = bf(np.random.standard_normal((DIM, J)) / np.sqrt(DIM) / u[None, :])
    g = np.random.standard_normal((B, S, H, QK)) * np.exp2(np.random.randint(-6, 1, (B, S, 1, 1))) * 4.0
    return {"x": x, "w": w, "freqs": bf(ang),
            "grad_out": bf(g / s[..., None] * ug[None, None])}


def reference(x, w, freqs, grad_out):
    g = f64(grad_out)
    gn = g[..., :NOPE].reshape(T, H * NOPE)
    gr = rope_backward(g[..., NOPE:], f64(freqs)).reshape(T, H * ROPE)
    dy = np.concatenate([gn, gr], axis=1)
    xf = f64(x).reshape(T, DIM)
    dx = mxq(dy, 1, "e5m2") @ mxq(f64(w), 1, "e4m3").T
    dw = mxq(xf, 0, "e4m3").T @ mxq(dy, 0, "e5m2")
    return dx.reshape(B, S, DIM), dw

@@ -1,0 +1,316 @@
+import math
+from contextlib import ExitStack
+
+import concourse.mybir as mybir
+from concourse.masks import make_identity
+
+F32 = mybir.dt.float32
+BF16 = mybir.dt.bfloat16
+U32 = mybir.dt.uint32
+U8 = mybir.dt.uint8
+E4M3 = mybir.dt.float8_e4m3fn_x4
+E5M2 = mybir.dt.float8_e5m2_x4
+ALU = mybir.AluOpType
+ACT = mybir.ActivationFunctionType
+
+P = 128
+DIM = 1536
+TOK = 1024
+J = 1536
+FLOPS = 2 * 2 * TOK * DIM * J
+
+LOADS = (
+    "G00 G01 G02 G03 W00 W01 W10 W11 W20 W21 G10 G11 G12 G13 X0 X1"
+)
+ORDER = (
+    "sort.0.0:V carg cos rA.0.0:V tn.0.0 tn.0.1 cn.0.0:S rA.0.1:V sort.0.1:S rB.0.0:V cn.0.1:S tn.0.2 tn.0.3 "
+    "cn.0.2:S tw.0.0.0 rB.0.1:V cn.0.3:S tw.0.1.0 cw.0.0.0:S tw.0.2.0 rC.0.0:V tw.0.0.1 cw.0.1.0:S tw.0.1.1 "
+    "cw.0.2.0:S rC.0.1:V tr.0.0 cw.0.0.1:S tw.0.2.1 cw.0.1.1:S cr.0.0:V tr.0.1 cw.0.2.1:S qD.0.0:V tw.1.0.0 "
+    "cr.0.1:S qD.0.1:V tw.1.0.1 cw.1.0.0:S tw.1.1.0 qD.0.2:V cw.1.0.1:S tw.1.1.1 qW.0.0:V cw.1.1.0:S tw.1.2.0 "
+    "qW.0.1:V cw.1.1.1:S tw.1.2.1 qW.0.2:V cw.1.2.0:S tw.2.0.0 cw.1.2.1:V A.0.0.0 cw.2.0.0:S qW.1.0:V qW.1.1:V "
+    "A.0.0.1 cA.0.0.0:S qW.1.2:V A.0.0.2 cA.0.0.1:S rA.1.0:V sort.1.0:S A.0.0.3 cA.0.0.2:V A.1.0.0 cA.0.0.3:S "
+    "rA.1.1:V sort.1.1:S A.1.0.1 cA.1.0.0:V A.1.0.2 cA.1.0.1:S rB.1.0:V A.1.0.3 cA.1.0.2:S rB.1.1:V tw.2.0.1 "
+    "cA.1.0.3:S tw.2.1.0 cw.2.0.1:S rC.1.0:V tw.2.1.1 cw.2.1.0:S tw.2.2.0 sA.0.0.0 cw.2.1.1:S qW.2.0:V tw.2.2.1 "
+    "sA.0.0.1 cw.2.2.0:S rC.1.1:V tn.1.0 sA.0.0.2 tn.1.1 cw.2.2.1:S tn.1.2 sA.0.0.3 cn.1.0:S qW.2.1:V tn.1.3 tr.1.0 "
+    "sA.1.0.0 cn.1.1:S qW.2.2:V tr.1.1 sA.1.0.1 cn.1.2:S cn.1.3:V A.2.0.0 sA.1.0.2 cr.1.0:S cr.1.1:V sA.1.0.3 "
+    "qD.1.0:V A.2.0.1 cA.2.0.0:S qD.1.1:V A.2.0.2 sA.2.0.0 cA.2.0.1:S qD.1.2:V A.2.0.3 sA.2.0.1 iX.0.0:V iX.1.0:S "
+    "A.0.1.0 cA.2.0.2:V A.0.1.1 cA.2.0.3:V sA.2.0.2 cA.0.1.0:V A.0.1.2 sA.2.0.3 cA.0.1.1:S iY.0.0:V sA.0.1.0 "
+    "A.0.1.3 cA.0.1.2:S sA.0.1.1 A.1.1.0 iY.1.0:V iY.0.1:S sA.0.1.2 A.1.1.1 cA.0.1.3:V A.1.1.2 cA.1.1.0:V sA.0.1.3 "
+    "cA.1.1.1:V A.1.1.3 sA.1.1.0 cA.1.1.2:S qX.0.0:V sA.1.1.1 A.2.1.0 cA.1.1.3:S qX.1.0:V sA.1.1.2 A.2.1.1 qY.0.0:V "
+    "sA.1.1.3 cA.2.1.0:S qY.1.0:V A.2.1.2 sA.2.1.0 cA.2.1.1:S iY.1.1:V A.2.1.3 sA.2.1.1 cA.2.1.2:S qY.0.1:V B.0.0 "
+    "sA.2.1.2 cA.2.1.3:S B.1.0 qY.1.1:V cB.0.0:S sA.2.1.3 B.2.0 iY.0.2:V cB.1.0:S B.0.1 cB.2.0:S B.1.1 iY.1.2:V "
+    "cB.0.1:S B.2.1 cB.1.1:S B.3.0 cB.2.1:S qY.0.2:V B.3.1 cB.3.0:S qY.1.2:V cB.3.1:S iX.0.1:V B.0.2 B.1.2 cB.0.2:S "
+    "B.2.2 iX.1.1:V cB.1.2:S sB.0 B.3.2 cB.2.2:S qX.0.1:V cB.3.2:S qX.1.1:V sB.1 iX.0.2:V iX.1.2:S B.4.0 B.4.1 sB.2 "
+    "B.4.2 cB.4.0:V B.5.0 cB.4.1:V B.5.1 cB.4.2:V cB.5.0:S sB.3 B.5.2 qX.0.2:V cB.5.1:S B.6.0 qX.1.2:V cB.5.2:S "
+    "B.6.1 cB.6.0:V sB.4 B.6.2 cB.6.1:S B.7.0 cB.6.2:V B.7.1 cB.7.0:S sB.5 B.7.2 cB.7.1:V B.8.0 cB.7.2:S B.8.1 "
+    "cB.8.0:V sB.6 B.8.2 cB.8.1:S B.9.0 cB.8.2:V B.9.1 sB.7 cB.9.0:S B.9.2 cB.9.1:V B.10.0 cB.9.2:S B.10.1 sB.8 "
+    "cB.10.0:V B.10.2 cB.10.1:S B.11.0 cB.10.2:V B.11.1 sB.9 cB.11.0:S B.11.2 cB.11.1:V cB.11.2:S sB.10 sB.11"
+)
+
+
+def tile_mla_pa_v_kernel(tc, x, w, freqs, grad_out, out_0, out_1):
+    nc = tc.nc
+    x_v = x.rearrange("(h b) s c -> h (b s) c", h=2).rearrange("h (p j) c -> h p j c", j=4)
+    g_v = grad_out.rearrange("(h b) s n q -> h (b s) (n q)", h=2).rearrange("h (p j) c -> h p j c", j=4)
+    w_v = w.rearrange("(n p j) c -> n p j c", n=3, j=4)
+    o0_v = out_0.rearrange("(h b) s c -> h (b s) c", h=2).rearrange("h (p j) c -> h p j c", j=4)
+    f_v = freqs.rearrange("(q j) f -> q (j f)", j=4)
+
+    with ExitStack() as ctx:
+        keep = ctx.enter_context(tc.tile_pool(name="keep", bufs=1))
+        stage = ctx.enter_context(tc.tile_pool(name="stage", bufs=2))
+        psum = ctx.enter_context(tc.psum_pool(name="psum", bufs=8))
+        ctx.enter_context(tc.manual_schedule())
+
+        ang = keep.tile([P, 4, 32], BF16, name="ang")
+        for r in range(4):
+            nc.sync.dma_start(out=ang[32 * r : 32 * r + 32, :, :].rearrange("p j f -> p (j f)"), in_=f_v)
+
+        g_t = [keep.tile([P, 4, 1536], BF16, name="g%d" % h) for h in range(2)]
+        x_t = [keep.tile([P, 4, 1536], BF16, name="x%d" % h) for h in range(2)]
+        w_t = {}
+        for name in LOADS.split(" "):
+            if name[0] == "G":
+                h, j = int(name[1]), int(name[2])
+                nc.sync.dma_start(out=g_t[h][:, j, :], in_=g_v[h, :, j, :])
+            elif name[0] == "W":
+                n, jp = int(name[1]), int(name[2])
+                t = stage.tile([P, 2, 1536], BF16, name="w_raw", bufs=3)
+                nc.sync.dma_start(out=t[:], in_=w_v[n, :, 2 * jp : 2 * jp + 2, :])
+                w_t[n, jp] = t
+            else:
+                h = int(name[1])
+                nc.sync.dma_start(out=x_t[h][:], in_=x_v[h])
+
+        ident = keep.tile([P, P], F32, name="ident")
+        make_identity(nc, ident[:])
+
+        absa = keep.tile([P, 128], F32, name="absa")
+        carg = keep.tile([P, 128], F32, name="carg")
+        cos2 = keep.tile([P, 4, 32, 2], F32, name="cos2")
+        sin2 = keep.tile([P, 4, 32, 2], F32, name="sin2")
+        nc.scalar.activation(out=absa[:], in_=ang[:].rearrange("p j f -> p (j f)"), func=ACT.Abs)
+        nc.scalar.activation(out=sin2[:, :, :, 0], in_=ang[:], func=ACT.Sin)
+        nc.scalar.activation(out=sin2[:, :, :, 1], in_=ang[:], func=ACT.Sin, scale=-1.0)
+
+        def t_carg():
+            nc.vector.tensor_scalar(out=carg[:], in0=absa[:], scalar1=-1.0, scalar2=math.pi / 2, op0=ALU.mult, op1=ALU.add)
+
+        def t_cos():
+            for e in range(2):
+                nc.scalar.activation(out=cos2[:, :, :, e], in_=carg[:].rearrange("p (j f) -> p j f", j=4), func=ACT.Sin)
+
+        dc = [keep.tile([P, 3, 512], U32, name="dc%d" % h, align_bytes=64) for h in range(2)]
+        ds = [keep.tile([P, 3, 512], U8, name="ds%d" % h, align_bytes=64) for h in range(2)]
+        wc = [keep.tile([P, 3, 512], U32, name="wc%d" % n, align_bytes=64) for n in range(3)]
+        ws = [keep.tile([P, 3, 512], U8, name="ws%d" % n, align_bytes=64) for n in range(3)]
+        xc = [keep.tile([P, 1536], U32, name="xc%d" % h, align_bytes=64) for h in range(2)]
+        xs = [keep.tile([P, 1536], U8, name="xs%d" % h, align_bytes=64) for h in range(2)]
+        yc = [keep.tile([P, 1536], U32, name="yc%d" % h, align_bytes=64) for h in range(2)]
+        ys = [keep.tile([P, 1536], U8, name="ys%d" % h, align_bytes=64) for h in range(2)]
+        rope = [keep.tile([P, 4, 512], BF16, name="rope%d" % h) for h in range(2)]
+        live = {}
+
+        def get(key, make):
+            if key not in live:
+                live[key] = make()
+            return live[key]
+
+        def grp():
+            t = stage.tile([P, 512, 4], BF16, name="grp", bufs=5, align_bytes=64)
+            return t
+
+        def dgn():
+            t = stage.tile([P, 2, 512, 4], BF16, name="dgn", bufs=1, align_bytes=64)
+            return t
+
+        def bank():
+            t = psum.tile([P, 512], F32, name="bank")
+            return t
+
+        def res0():
+            t = stage.tile([P, 512], F32, name="res_0", bufs=4)
+            return t
+
+        def res1():
+            t = stage.tile([P, 1536], F32, name="res_1", bufs=5)
+            return t
+
+        def srtd():
+            t = stage.tile([P, 2, 2, 2, 128], F32, name="sorted", bufs=2)
+            return t
+
+        def rota():
+            t = stage.tile([P, 2, 8, 64], F32, name="rot_a", bufs=2)
+            return t
+
+        def rotb():
+            t = stage.tile([P, 2, 8, 64], F32, name="rot_b", bufs=2)
+            return t
+
+        def words(t):
+            return t.rearrange("p c t -> p (c t)").bitcast(F32).rearrange("p (c u) -> p c u", u=2)
+
+        def copy_out(eng, out, in_):
+            if eng == "S":
+                nc.scalar.copy(out=out, in_=in_)
+            else:
+                nc.vector.tensor_copy(out=out, in_=in_)
+
+        def quant(codes, fmt, scales, in_):
+            nc.vector.quantize_mx(out=codes.bitcast(fmt), scales=scales, in_=in_.rearrange("p c t -> p (c t)"))
+
+        def t_sort(eng, h, jj):
+            srt = get(("sort", h, jj), srtd)
+            gw = g_t[h][:, 2 * jj : 2 * jj + 2, :].rearrange("p j c -> p (j c)").bitcast(F32)
+            gw = gw.rearrange("p (a n q) -> p a n q", a=4, n=4)[:, :, :, 0:64]
+            so = srt[:].rearrange("p j q u (n i) -> p (j q) u n i", n=4)
+            for u in range(2):
+                copy_out(eng, so[:, :, u], gw[:, :, :, u::2])
+
+        def t_tn(h, j):
+            srt = get(("sort", h, j // 2), srtd)
+            b = get(("tn", h, j), bank)
+            bv = b[:].rearrange("p (q u r) -> p q u r", q=2, u=2)
+            for q in range(2):
+                for u in range(2):
+                    nc.tensor.transpose(bv[:, q, u, :], srt[:, j % 2, q, u, :], ident[:])
+
+        def t_cn(eng, h, j):
+            dg = get(("dgn", h), dgn)
+            dgw = dg[:].rearrange("p q c t -> p (q c t)").bitcast(F32).rearrange("p (q c u) -> p q c u", q=2, u=2)
+            bv = get(("tn", h, j), bank)[:].rearrange("p (q u r) -> p q u r", q=2, u=2)
+            copy_out(eng, dgw[:, :, j * 128 : j * 128 + 128, :], bv.rearrange("p q u r -> p q r u"))
+
+        def t_qd(h, q):
+            if q < 2:
+                quant(dc[h][:, q, :], E5M2, ds[h][:, q, :], get(("dgn", h), dgn)[:, q])
+            else:
+                quant(dc[h][:, 2, :], E5M2, ds[h][:, 2, :], get(("dr", h), grp)[:])
+
+        def rope_of(h, js):
+            return g_t[h][:, js, :].rearrange("p j (n q) -> p j n q", q=192)[:, :, :, 128:]
+
+        def t_ra(h, jj):
+            js = slice(2 * jj, 2 * jj + 2)
+            c2 = cos2[:, js].rearrange("p j f e -> p j (f e)").unsqueeze(2).to_broadcast([P, 2, 8, 64])
+            nc.vector.tensor_tensor(out=get(("ra", h, jj), rota)[:], in0=rope_of(h, js), in1=c2, op=ALU.mult)
+
+        def t_rb(h, jj):
+            gr = rope_of(h, slice(2 * jj, 2 * jj + 2))
+            b = get(("rb", h, jj), rotb)
+            for i in range(2):
+                swapped = gr[:, i].rearrange("p n (f e) -> p n f e", e=2)[:, :, :, ::-1]
+                s2 = sin2[:, 2 * jj + i].unsqueeze(1).to_broadcast([P, 8, 32, 2])
+                nc.vector.tensor_tensor(out=b[:, i].rearrange("p n (f e) -> p n f e", e=2), in0=swapped, in1=s2, op=ALU.mult)
+
+        def t_rc(h, jj):
+            nc.vector.tensor_tensor(
+                out=rope[h][:, 2 * jj : 2 * jj + 2, :],
+                in0=get(("ra", h, jj), rota)[:].rearrange("p j n q -> p j (n q)"),
+                in1=get(("rb", h, jj), rotb)[:].rearrange("p j n q -> p j (n q)"),
+                op=ALU.add,
+            )
+
+        def t_tr(h, jj):
+            bv = get(("tr", h, jj), bank)[:].rearrange("p (j u r) -> p j u r", j=2, u=2)
+            rw = rope[h][:].rearrange("p j c -> p (j c)").bitcast(F32).rearrange("p (j c) -> p j c", j=4)
+            for i in range(2):
+                for u in range(2):
+                    nc.tensor.transpose(bv[:, i, u, :], rw[:, 2 * jj + i, u::2], ident[:])
+
+        def halves(dst, jp, b):
+            out = words(dst)[:, jp * 256 : jp * 256 + 256, :].rearrange("p (j r) u -> p j r u", j=2)
+            return out, b[:].rearrange("p (j u r) -> p j r u", j=2, u=2)
+
+        def t_cr(eng, h, jj):
+            o, i = halves(get(("dr", h), grp)[:], jj, get(("tr", h, jj), bank))
+            copy_out(eng, o, i)
+
+        def t_tw(n, q, jp):
+            ww = w_t[n, jp][:].rearrange("p j c -> p (j c)").bitcast(F32).rearrange("p (j c) -> p j c", j=2)
+            bv = get(("tw", n, q, jp), bank)[:].rearrange("p (j u r) -> p j u r", j=2, u=2)
+            for i in range(2):
+                for u in range(2):
+                    nc.tensor.transpose(bv[:, i, u, :], ww[:, i, 256 * q + u : 256 * q + 256 : 2], ident[:])
+
+        def t_cw(eng, n, q, jp):
+            o, i = halves(get(("wg", n, q), grp)[:], jp, get(("tw", n, q, jp), bank))
+            copy_out(eng, o, i)
+
+        def t_qw(n, q):
+            quant(wc[n][:, q, :], E4M3, ws[n][:, q, :], get(("wg", n, q), grp)[:])
+
+        def t_a(n, h, j):
+            acc = get(("a", n, h, j), bank)
+            cols = slice(j * 128, j * 128 + 128)
+            for q in range(3):
+                nc.tensor.matmul_mx(
+                    out=acc[:],
+                    lhsT=dc[h][:, q, cols].bitcast(E5M2),
+                    lhsT_scale=ds[h][:, q, cols],
+                    rhs=wc[n][:, q, :].bitcast(E4M3),
+                    rhs_scale=ws[n][:, q, :],
+                    start=(q == 0),
+                    stop=(q == 2),
+                )
+
+        def t_ca(eng, n, h, j):
+            res = get(("ra0", n, h, j), res0)
+            copy_out(eng, res[:].rearrange("p (r j) -> p r j", j=4), get(("a", n, h, j), bank)[:].rearrange("p (j r) -> p r j", j=4))
+
+        def t_sa(n, h, j):
+            nc.sync.dma_start(out=o0_v[h, :, j, n * 512 : n * 512 + 512], in_=get(("ra0", n, h, j), res0)[:])
+
+        def t_ix(eng, h, c):
+            copy_out(eng, get(("xg", h, c), grp)[:].rearrange("p (c i) t -> p c t i", i=4),
+                     x_t[h][:, :, c * 512 : c * 512 + 512].rearrange("p t (c i) -> p c t i", i=4))
+
+        def t_qx(h, c):
+            cs = slice(c * 512, c * 512 + 512)
+            quant(xc[h][:, cs], E4M3, xs[h][:, cs], get(("xg", h, c), grp)[:])
+
+        def t_iy(eng, h, c):
+            yg = get(("yg", h, c), grp)
+            if c < 2:
+                src = g_t[h][:, :, c * 768 : c * 768 + 768].rearrange("p t (n q) -> p t n q", n=4)[:, :, :, 0:128]
+                copy_out(eng, yg[:].rearrange("p (n k) t -> p n k t", n=4), src.rearrange("p t n k -> p n k t"))
+            else:
+                copy_out(eng, yg[:].rearrange("p (c i) t -> p c t i", i=4), rope[h][:].rearrange("p t (c i) -> p c t i", i=4))
+
+        def t_qy(h, c):
+            cs = slice(c * 512, c * 512 + 512)
+            quant(yc[h][:, cs], E5M2, ys[h][:, cs], get(("yg", h, c), grp)[:])
+
+        def t_b(m, n):
+            acc = get(("b", m, n), bank)
+            cols = slice(m * 128, m * 128 + 128)
+            ns = slice(n * 512, n * 512 + 512)
+            for h in range(2):
+                nc.tensor.matmul_mx(
+                    out=acc[:],
+                    lhsT=xc[h][:, cols].bitcast(E4M3),
+                    lhsT_scale=xs[h][:, cols],
+                    rhs=yc[h][:, ns].bitcast(E5M2),
+                    rhs_scale=ys[h][:, ns],
+                    start=(h == 0),
+                    stop=(h == 1),
+                )
+
+        def t_cb(eng, m, n):
+            copy_out(eng, get(("rb1", m), res1)[:, n * 512 : n * 512 + 512], get(("b", m, n), bank)[:])
+
+        def t_sb(m):
+            nc.sync.dma_start(out=out_1[m * 128 : m * 128 + 128, :], in_=get(("rb1", m), res1)[:])
+
+        fns = {"carg": t_carg, "cos": t_cos, "sort": t_sort, "tn": t_tn, "cn": t_cn, "qD": t_qd, "rA": t_ra, "rB": t_rb, "rC": t_rc, "tr": t_tr, "cr": t_cr,
+               "tw": t_tw, "cw": t_cw, "qW": t_qw, "A": t_a, "cA": t_ca, "sA": t_sa, "iX": t_ix, "qX": t_qx, "iY": t_iy,
+               "qY": t_qy, "B": t_b, "cB": t_cb, "sB": t_sb}
+        for tok in ORDER.split(" "):
+            parts = tok.split(":")
+            f = parts[0].split(".")
+            args = [int(a) for a in f[1:]]
+            if len(parts) == 2 and f[0] in ("sort", "cn", "cr", "cw", "cA", "iX", "iY", "cB"):
+                fns[f[0]](parts[1], *args)
+            else:
+                fns[f[0]](*args)

@@ -20,31 +20,33 @@ J = 1536
 FLOPS = 2 * 2 * TOK * DIM * J
 
 LOADS = (
-    "G00 G01 G02 G03 W00 W01 W10 W11 W20 W21 G10 G11 G12 G13 X0 X1"
+    "G00 G01 G02 G03 W00 W01 G10 G11 G12 G13 W10 W11 W20 W21 X0 X1"
 )
 ORDER = (
-    "sort.0.0:V carg cos rA.0.0:V tn.0.0 tn.0.1 cn.0.0:S rA.0.1:V sort.0.1:S rB.0.0:V cn.0.1:S tn.0.2 tn.0.3 "
-    "cn.0.2:S tw.0.0.0 rB.0.1:V cn.0.3:S tw.0.1.0 cw.0.0.0:S tw.0.2.0 rC.0.0:V tw.0.0.1 cw.0.1.0:S tw.0.1.1 "
-    "cw.0.2.0:S rC.0.1:V tr.0.0 cw.0.0.1:S tw.0.2.1 cw.0.1.1:S cr.0.0:V tr.0.1 cw.0.2.1:S qD.0.0:V tw.1.0.0 "
-    "cr.0.1:S qD.0.1:V tw.1.0.1 cw.1.0.0:S tw.1.1.0 qD.0.2:V cw.1.0.1:S tw.1.1.1 qW.0.0:V cw.1.1.0:S tw.1.2.0 "
-    "qW.0.1:V cw.1.1.1:S tw.1.2.1 qW.0.2:V cw.1.2.0:S tw.2.0.0 cw.1.2.1:V A.0.0.0 cw.2.0.0:S qW.1.0:V qW.1.1:V "
-    "A.0.0.1 cA.0.0.0:S qW.1.2:V A.0.0.2 cA.0.0.1:S rA.1.0:V sort.1.0:S A.0.0.3 cA.0.0.2:V A.1.0.0 cA.0.0.3:S "
-    "rA.1.1:V sort.1.1:S A.1.0.1 cA.1.0.0:V A.1.0.2 cA.1.0.1:S rB.1.0:V A.1.0.3 cA.1.0.2:S rB.1.1:V tw.2.0.1 "
-    "cA.1.0.3:S tw.2.1.0 cw.2.0.1:S rC.1.0:V tw.2.1.1 cw.2.1.0:S tw.2.2.0 sA.0.0.0 cw.2.1.1:S qW.2.0:V tw.2.2.1 "
-    "sA.0.0.1 cw.2.2.0:S rC.1.1:V tn.1.0 sA.0.0.2 tn.1.1 cw.2.2.1:S tn.1.2 sA.0.0.3 cn.1.0:S qW.2.1:V tn.1.3 tr.1.0 "
-    "sA.1.0.0 cn.1.1:S qW.2.2:V tr.1.1 sA.1.0.1 cn.1.2:S cn.1.3:V A.2.0.0 sA.1.0.2 cr.1.0:S cr.1.1:V sA.1.0.3 "
-    "qD.1.0:V A.2.0.1 cA.2.0.0:S qD.1.1:V A.2.0.2 sA.2.0.0 cA.2.0.1:S qD.1.2:V A.2.0.3 sA.2.0.1 iX.0.0:V iX.1.0:S "
-    "A.0.1.0 cA.2.0.2:V A.0.1.1 cA.2.0.3:V sA.2.0.2 cA.0.1.0:V A.0.1.2 sA.2.0.3 cA.0.1.1:S iY.0.0:V sA.0.1.0 "
-    "A.0.1.3 cA.0.1.2:S sA.0.1.1 A.1.1.0 iY.1.0:V iY.0.1:S sA.0.1.2 A.1.1.1 cA.0.1.3:V A.1.1.2 cA.1.1.0:V sA.0.1.3 "
-    "cA.1.1.1:V A.1.1.3 sA.1.1.0 cA.1.1.2:S qX.0.0:V sA.1.1.1 A.2.1.0 cA.1.1.3:S qX.1.0:V sA.1.1.2 A.2.1.1 qY.0.0:V "
-    "sA.1.1.3 cA.2.1.0:S qY.1.0:V A.2.1.2 sA.2.1.0 cA.2.1.1:S iY.1.1:V A.2.1.3 sA.2.1.1 cA.2.1.2:S qY.0.1:V B.0.0 "
-    "sA.2.1.2 cA.2.1.3:S B.1.0 qY.1.1:V cB.0.0:S sA.2.1.3 B.2.0 iY.0.2:V cB.1.0:S B.0.1 cB.2.0:S B.1.1 iY.1.2:V "
-    "cB.0.1:S B.2.1 cB.1.1:S B.3.0 cB.2.1:S qY.0.2:V B.3.1 cB.3.0:S qY.1.2:V cB.3.1:S iX.0.1:V B.0.2 B.1.2 cB.0.2:S "
-    "B.2.2 iX.1.1:V cB.1.2:S sB.0 B.3.2 cB.2.2:S qX.0.1:V cB.3.2:S qX.1.1:V sB.1 iX.0.2:V iX.1.2:S B.4.0 B.4.1 sB.2 "
-    "B.4.2 cB.4.0:V B.5.0 cB.4.1:V B.5.1 cB.4.2:V cB.5.0:S sB.3 B.5.2 qX.0.2:V cB.5.1:S B.6.0 qX.1.2:V cB.5.2:S "
-    "B.6.1 cB.6.0:V sB.4 B.6.2 cB.6.1:S B.7.0 cB.6.2:V B.7.1 cB.7.0:S sB.5 B.7.2 cB.7.1:V B.8.0 cB.7.2:S B.8.1 "
-    "cB.8.0:V sB.6 B.8.2 cB.8.1:S B.9.0 cB.8.2:V B.9.1 sB.7 cB.9.0:S B.9.2 cB.9.1:V B.10.0 cB.9.2:S B.10.1 sB.8 "
-    "cB.10.0:V B.10.2 cB.10.1:S B.11.0 cB.10.2:V B.11.1 sB.9 cB.11.0:S B.11.2 cB.11.1:V cB.11.2:S sB.10 sB.11"
+    "warm.5 sort.0.0:V carg cos rA.0.0:V tn.0.0 warm.1 tn.0.1 warm.1 sort.0.1:S rA.0.1:V cn.0.0:S rB.0.0:V tn.0.2 "
+    "warm.1 cn.0.1:S tn.0.3 warm.1 tw.0.0.0 warm.1 cn.0.2:S rB.0.1:V tw.0.1.0 warm.1 cn.0.3:S tw.0.0.1 warm.1 "
+    "rC.0.0:V cw.0.0.0:S tw.0.1.1 warm.1 cw.0.1.0:S rC.0.1:V tw.0.2.0 warm.1 cw.0.0.1:S tr.0.0 warm.1 cw.0.1.1:S "
+    "qD.0.0:V tw.0.2.1 warm.1 cw.0.2.0:S tr.0.1 warm.1 cr.0.0:S cw.0.2.1:V sort.1.0:S cr.0.1:V tw.1.0.0 warm.1 "
+    "qW.0.0:V tw.1.1.0 warm.1 sort.1.1:S qD.0.2:V tn.1.0 warm.1 tn.1.1 warm.1 qW.0.1:V cw.1.0.0:S tw.1.0.1 warm.1 "
+    "qW.0.2:V cn.1.0:S tn.1.2 warm.1 rA.1.0:V tn.1.3 warm.1 cn.1.1:S A.0.0.0 cn.1.2:S rA.1.1:V cn.1.3:S A.0.0.1 "
+    "cA.0.0.0:S rB.1.0:V A.0.0.2 cw.1.0.1:S cA.0.0.1:S A.0.0.3 rB.1.1:V cA.0.0.2:S tw.1.1.1 cA.0.0.3:S rC.1.0:V "
+    "tw.1.2.0 cw.1.1.0:S tw.1.2.1 tw.2.0.0 rC.1.1:V cw.1.1.1:S tr.1.0 cw.1.2.0:S tw.2.0.1 qD.1.0:V sA.0.0.0 "
+    "cw.1.2.1:S tr.1.1 sA.0.0.1 cr.1.0:S tw.2.1.0 sA.0.0.2 qW.1.0:V tw.2.1.1 cr.1.1:S sA.0.0.3 qW.1.1:V tw.2.2.0 "
+    "cw.2.0.0:S tw.2.2.1 qD.1.2:V cw.2.0.1:S qW.1.2:V cw.2.1.0:S A.0.1.0 qW.2.0:V cw.2.1.1:S A.0.1.1 iX.0.0:V "
+    "cw.2.2.0:S A.0.1.2 cA.0.1.0:S qW.2.1:V cA.0.1.1:S A.0.1.3 sA.0.1.0 iX.1.0:V cA.0.1.2:S sA.0.1.1 A.1.0.0 "
+    "cA.0.1.3:S sA.0.1.2 A.1.0.1 iY.0.0:V cw.2.2.1:S sA.0.1.3 A.1.0.2 cA.1.0.0:S qW.2.2:V cA.1.0.1:S A.1.0.3 "
+    "sA.1.0.0 cA.1.0.2:S iY.1.0:V sA.1.0.1 A.1.1.0 cA.1.0.3:S sA.1.0.2 A.1.1.1 qX.0.0:V cA.1.1.0:S sA.1.0.3 A.1.1.2 "
+    "qX.1.0:V cA.1.1.1:S sA.1.1.0 qY.0.0:V A.1.1.3 cA.1.1.2:S sA.1.1.1 qY.1.0:V A.2.0.0 cA.1.1.3:S iY.0.1:V "
+    "sA.1.1.2 A.2.0.1 cA.2.0.0:S sA.1.1.3 A.2.0.2 iY.1.1:V iY.0.2:S sA.2.0.0 A.2.0.3 cA.2.0.1:V A.2.1.0 cA.2.0.2:V "
+    "sA.2.0.1 A.2.1.1 qY.0.1:V cA.2.0.3:S sA.2.0.2 A.2.1.2 qY.1.1:V cA.2.1.0:S sA.2.0.3 cA.2.1.1:S iY.1.2:V A.2.1.3 "
+    "sA.2.1.0 cA.2.1.2:S sA.2.1.1 B.0.0 cA.2.1.3:S qY.0.2:V B.0.1 sA.2.1.2 cB.0.0:S qY.1.2:V B.1.0 sA.2.1.3 "
+    "cB.0.1:S B.1.1 iX.0.1:V B.0.2 cB.1.0:S B.1.2 cB.1.1:S iX.1.1:V B.2.0 cB.0.2:S B.2.1 cB.1.2:S cB.2.0:V B.2.2 "
+    "sB.0 cB.2.1:S B.3.0 qX.0.1:V cB.2.2:S B.3.1 qX.1.1:V B.3.2 sB.1 cB.3.0:S iX.0.2:V B.4.0 cB.3.1:S B.4.1 "
+    "cB.3.2:S cB.4.0:V sB.2 B.4.2 cB.4.1:S B.5.0 iX.1.2:V cB.4.2:S B.5.1 sB.3 cB.5.0:S B.5.2 qX.0.2:V B.6.0 "
+    "cB.5.1:S qX.1.2:V B.6.1 cB.5.2:S sB.4 B.6.2 cB.6.0:S cB.6.1:V B.7.0 cB.6.2:S B.7.1 sB.5 cB.7.0:S B.7.2 "
+    "cB.7.1:S B.8.0 B.8.1 cB.7.2:S sB.6 cB.8.0:V B.8.2 cB.8.1:S B.9.0 cB.8.2:S B.9.1 sB.7 cB.9.0:S B.9.2 B.10.0 "
+    "cB.9.1:S cB.9.2:V B.10.1 sB.8 cB.10.0:S B.10.2 cB.10.1:S B.11.0 cB.10.2:S B.11.1 sB.9 B.11.2 cB.11.0:S "
+    "cB.11.1:V cB.11.2:S sB.10.0 sB.10.1 sB.10.2 sB.11.0 sB.11.1 sB.11.2"
 )
 
 
@@ -83,7 +85,6 @@ def tile_mla_pa_v_kernel(tc, x, w, freqs, grad_out, out_0, out_1):
                 nc.sync.dma_start(out=x_t[h][:], in_=x_v[h])
 
         ident = keep.tile([P, P], F32, name="ident")
-        make_identity(nc, ident[:])
 
         absa = keep.tile([P, 128], F32, name="absa")
         carg = keep.tile([P, 128], F32, name="carg")
@@ -151,6 +152,15 @@ def tile_mla_pa_v_kernel(tc, x, w, freqs, grad_out, out_0, out_1):
         def words(t):
             return t.rearrange("p c t -> p (c t)").bitcast(F32).rearrange("p (c u) -> p c u", u=2)
 
+        warm_in = keep.tile([P, 512], BF16, name="warm_in")
+        nc.gpsimd.memset(warm_in[:], 0.0)
+        make_identity(nc, ident[:])
+
+        def t_warm(k):
+            b = get("warm", bank)
+            for i in range(k):
+                nc.tensor.matmul(b[:], warm_in[:, 0:128], warm_in[:], start=True, stop=True)
+
         def copy_out(eng, out, in_):
             if eng == "S":
                 nc.scalar.copy(out=out, in_=in_)
@@ -165,8 +175,11 @@ def tile_mla_pa_v_kernel(tc, x, w, freqs, grad_out, out_0, out_1):
             gw = g_t[h][:, 2 * jj : 2 * jj + 2, :].rearrange("p j c -> p (j c)").bitcast(F32)
             gw = gw.rearrange("p (a n q) -> p a n q", a=4, n=4)[:, :, :, 0:64]
             so = srt[:].rearrange("p j q u (n i) -> p (j q) u n i", n=4)
-            for u in range(2):
-                copy_out(eng, so[:, :, u], gw[:, :, :, u::2])
+            if eng == "V":
+                copy_out(eng, so, gw.rearrange("p a n (i u) -> p a u n i", u=2))
+            else:
+                for u in range(2):
+                    copy_out(eng, so[:, :, u], gw[:, :, :, u::2])
 
         def t_tn(h, j):
             srt = get(("sort", h, j // 2), srtd)
@@ -183,8 +196,9 @@ def tile_mla_pa_v_kernel(tc, x, w, freqs, grad_out, out_0, out_1):
             copy_out(eng, dgw[:, :, j * 128 : j * 128 + 128, :], bv.rearrange("p q u r -> p q r u"))
 
         def t_qd(h, q):
-            if q < 2:
-                quant(dc[h][:, q, :], E5M2, ds[h][:, q, :], get(("dgn", h), dgn)[:, q])
+            if q == 0:
+                quant(dc[h][:, 0:2, :].rearrange("p q c -> p (q c)"), E5M2, ds[h][:, 0:2, :].rearrange("p q c -> p (q c)"),
+                      get(("dgn", h), dgn)[:].rearrange("p q c t -> p (q c) t"))
             else:
                 quant(dc[h][:, 2, :], E5M2, ds[h][:, 2, :], get(("dr", h), grp)[:])
 
@@ -199,10 +213,9 @@ def tile_mla_pa_v_kernel(tc, x, w, freqs, grad_out, out_0, out_1):
         def t_rb(h, jj):
             gr = rope_of(h, slice(2 * jj, 2 * jj + 2))
             b = get(("rb", h, jj), rotb)
-            for i in range(2):
-                swapped = gr[:, i].rearrange("p n (f e) -> p n f e", e=2)[:, :, :, ::-1]
-                s2 = sin2[:, 2 * jj + i].unsqueeze(1).to_broadcast([P, 8, 32, 2])
-                nc.vector.tensor_tensor(out=b[:, i].rearrange("p n (f e) -> p n f e", e=2), in0=swapped, in1=s2, op=ALU.mult)
+            swapped = gr.rearrange("p j n (f e) -> p j n f e", e=2)[:, :, :, :, ::-1]
+            s2 = sin2[:, 2 * jj : 2 * jj + 2].unsqueeze(2).to_broadcast([P, 2, 8, 32, 2])
+            nc.vector.tensor_tensor(out=b[:].rearrange("p j n (f e) -> p j n f e", e=2), in0=swapped, in1=s2, op=ALU.mult)
 
         def t_rc(h, jj):
             nc.vector.tensor_tensor(
@@ -300,10 +313,11 @@ def tile_mla_pa_v_kernel(tc, x, w, freqs, grad_out, out_0, out_1):
         def t_cb(eng, m, n):
             copy_out(eng, get(("rb1", m), res1)[:, n * 512 : n * 512 + 512], get(("b", m, n), bank)[:])
 
-        def t_sb(m):
-            nc.sync.dma_start(out=out_1[m * 128 : m * 128 + 128, :], in_=get(("rb1", m), res1)[:])
+        def t_sb(m, n=None):
+            cs = slice(0, 1536) if n is None else slice(n * 512, n * 512 + 512)
+            nc.sync.dma_start(out=out_1[m * 128 : m * 128 + 128, cs], in_=get(("rb1", m), res1)[:, cs])
 
-        fns = {"carg": t_carg, "cos": t_cos, "sort": t_sort, "tn": t_tn, "cn": t_cn, "qD": t_qd, "rA": t_ra, "rB": t_rb, "rC": t_rc, "tr": t_tr, "cr": t_cr,
+        fns = {"warm": t_warm, "carg": t_carg, "cos": t_cos, "sort": t_sort, "tn": t_tn, "cn": t_cn, "qD": t_qd, "rA": t_ra, "rB": t_rb, "rC": t_rc, "tr": t_tr, "cr": t_cr,
                "tw": t_tw, "cw": t_cw, "qW": t_qw, "A": t_a, "cA": t_ca, "sA": t_sa, "iX": t_ix, "qX": t_qx, "iY": t_iy,
                "qY": t_qy, "B": t_b, "cB": t_cb, "sB": t_sb}
         for tok in ORDER.split(" "):

@@ -20,33 +20,34 @@ J = 1536
 FLOPS = 2 * 2 * TOK * DIM * J
 
 LOADS = (
-    "G00 G01 G02 G03 W00 W01 G10 G11 G12 G13 W10 W11 W20 W21 X0 X1"
+    "G00 G01 G02 G03 W00 W01 W10 W11 W20 W21 G10 G11 G12 G13 X0 X1"
 )
 ORDER = (
-    "warm.5 sort.0.0:V carg cos rA.0.0:V tn.0.0 warm.1 tn.0.1 warm.1 sort.0.1:S rA.0.1:V cn.0.0:S rB.0.0:V tn.0.2 "
-    "warm.1 cn.0.1:S tn.0.3 warm.1 tw.0.0.0 warm.1 cn.0.2:S rB.0.1:V tw.0.1.0 warm.1 cn.0.3:S tw.0.0.1 warm.1 "
-    "rC.0.0:V cw.0.0.0:S tw.0.1.1 warm.1 cw.0.1.0:S rC.0.1:V tw.0.2.0 warm.1 cw.0.0.1:S tr.0.0 warm.1 cw.0.1.1:S "
-    "qD.0.0:V tw.0.2.1 warm.1 cw.0.2.0:S tr.0.1 warm.1 cr.0.0:S cw.0.2.1:V sort.1.0:S cr.0.1:V tw.1.0.0 warm.1 "
-    "qW.0.0:V tw.1.1.0 warm.1 sort.1.1:S qD.0.2:V tn.1.0 warm.1 tn.1.1 warm.1 qW.0.1:V cw.1.0.0:S tw.1.0.1 warm.1 "
-    "qW.0.2:V cn.1.0:S tn.1.2 warm.1 rA.1.0:V tn.1.3 warm.1 cn.1.1:S A.0.0.0 cn.1.2:S rA.1.1:V cn.1.3:S A.0.0.1 "
-    "cA.0.0.0:S rB.1.0:V A.0.0.2 cw.1.0.1:S cA.0.0.1:S A.0.0.3 rB.1.1:V cA.0.0.2:S tw.1.1.1 cA.0.0.3:S rC.1.0:V "
-    "tw.1.2.0 cw.1.1.0:S tw.1.2.1 tw.2.0.0 rC.1.1:V cw.1.1.1:S tr.1.0 cw.1.2.0:S tw.2.0.1 qD.1.0:V sA.0.0.0 "
-    "cw.1.2.1:S tr.1.1 sA.0.0.1 cr.1.0:S tw.2.1.0 sA.0.0.2 qW.1.0:V tw.2.1.1 cr.1.1:S sA.0.0.3 qW.1.1:V tw.2.2.0 "
-    "cw.2.0.0:S tw.2.2.1 qD.1.2:V cw.2.0.1:S qW.1.2:V cw.2.1.0:S A.0.1.0 qW.2.0:V cw.2.1.1:S A.0.1.1 iX.0.0:V "
-    "cw.2.2.0:S A.0.1.2 cA.0.1.0:S qW.2.1:V cA.0.1.1:S A.0.1.3 sA.0.1.0 iX.1.0:V cA.0.1.2:S sA.0.1.1 A.1.0.0 "
-    "cA.0.1.3:S sA.0.1.2 A.1.0.1 iY.0.0:V cw.2.2.1:S sA.0.1.3 A.1.0.2 cA.1.0.0:S qW.2.2:V cA.1.0.1:S A.1.0.3 "
-    "sA.1.0.0 cA.1.0.2:S iY.1.0:V sA.1.0.1 A.1.1.0 cA.1.0.3:S sA.1.0.2 A.1.1.1 qX.0.0:V cA.1.1.0:S sA.1.0.3 A.1.1.2 "
-    "qX.1.0:V cA.1.1.1:S sA.1.1.0 qY.0.0:V A.1.1.3 cA.1.1.2:S sA.1.1.1 qY.1.0:V A.2.0.0 cA.1.1.3:S iY.0.1:V "
-    "sA.1.1.2 A.2.0.1 cA.2.0.0:S sA.1.1.3 A.2.0.2 iY.1.1:V iY.0.2:S sA.2.0.0 A.2.0.3 cA.2.0.1:V A.2.1.0 cA.2.0.2:V "
-    "sA.2.0.1 A.2.1.1 qY.0.1:V cA.2.0.3:S sA.2.0.2 A.2.1.2 qY.1.1:V cA.2.1.0:S sA.2.0.3 cA.2.1.1:S iY.1.2:V A.2.1.3 "
-    "sA.2.1.0 cA.2.1.2:S sA.2.1.1 B.0.0 cA.2.1.3:S qY.0.2:V B.0.1 sA.2.1.2 cB.0.0:S qY.1.2:V B.1.0 sA.2.1.3 "
-    "cB.0.1:S B.1.1 iX.0.1:V B.0.2 cB.1.0:S B.1.2 cB.1.1:S iX.1.1:V B.2.0 cB.0.2:S B.2.1 cB.1.2:S cB.2.0:V B.2.2 "
-    "sB.0 cB.2.1:S B.3.0 qX.0.1:V cB.2.2:S B.3.1 qX.1.1:V B.3.2 sB.1 cB.3.0:S iX.0.2:V B.4.0 cB.3.1:S B.4.1 "
-    "cB.3.2:S cB.4.0:V sB.2 B.4.2 cB.4.1:S B.5.0 iX.1.2:V cB.4.2:S B.5.1 sB.3 cB.5.0:S B.5.2 qX.0.2:V B.6.0 "
-    "cB.5.1:S qX.1.2:V B.6.1 cB.5.2:S sB.4 B.6.2 cB.6.0:S cB.6.1:V B.7.0 cB.6.2:S B.7.1 sB.5 cB.7.0:S B.7.2 "
-    "cB.7.1:S B.8.0 B.8.1 cB.7.2:S sB.6 cB.8.0:V B.8.2 cB.8.1:S B.9.0 cB.8.2:S B.9.1 sB.7 cB.9.0:S B.9.2 B.10.0 "
-    "cB.9.1:S cB.9.2:V B.10.1 sB.8 cB.10.0:S B.10.2 cB.10.1:S B.11.0 cB.10.2:S B.11.1 sB.9 B.11.2 cB.11.0:S "
-    "cB.11.1:V cB.11.2:S sB.10.0 sB.10.1 sB.10.2 sB.11.0 sB.11.1 sB.11.2"
+    "warm.5 sort.0.0:V carg cos rA.0.0:V tn.0.0 warm.1 tn.0.1 warm.1 cn.0.0:S rA.0.1:V sort.0.1:S rB.0.0:V tw.0.0.0 "
+    "warm.1 cn.0.1:S tw.0.1.0 warm.1 rB.0.1:V cw.0.0.0:S tw.0.2.0 warm.1 cw.0.1.0:S tw.0.0.1 warm.1 rC.0.0:V "
+    "cw.0.2.0:S tw.0.1.1 warm.1 cw.0.0.1:S tw.0.2.1 warm.1 rC.0.1:V cw.0.1.1:S tn.0.2 warm.1 cw.0.2.1:S tn.0.3 "
+    "warm.1 qW.0.0:V tr.0.0 warm.1 cn.0.2:S cn.0.3:V tr.0.1 warm.1 cr.0.0:S qW.0.1:V tw.1.0.0 warm.1 cr.0.1:S "
+    "qD.0.0:V tw.1.0.1 warm.1 cw.1.0.0:S tw.1.1.0 warm.1 cw.1.0.1:S qD.0.2:V tw.1.1.1 warm.1 cw.1.1.0:S qW.0.2:V "
+    "tw.1.2.0 warm.1 cw.1.1.1:S qW.1.0:V tw.1.2.1 warm.1 cw.1.2.0:S rA.1.0:V A.0.0.0 sort.1.0:S rB.1.0:V A.0.0.1 "
+    "cA.0.0.0:S A.0.0.2 rA.1.1:V sort.1.1:S A.0.0.3 cA.0.0.1:V cA.0.0.2:S tn.1.0 rB.1.1:V tn.1.1 cA.0.0.3:S tn.1.2 "
+    "cn.1.0:S tn.1.3 tw.2.0.0 rC.1.0:V cn.1.1:S tw.2.0.1 cn.1.2:S tw.2.1.0 rC.1.1:V tr.1.0 cn.1.3:S sA.0.0.0 "
+    "tw.2.1.1 cw.1.2.1:S sA.0.0.1 qW.1.1:V tw.2.2.0 cr.1.0:S sA.0.0.2 qD.1.0:V tr.1.1 sA.0.0.3 cw.2.0.0:S tw.2.2.1 "
+    "cr.1.1:S qW.1.2:V cw.2.0.1:S iX.0.0:V A.1.0.0 cw.2.1.0:S cw.2.1.1:S A.1.0.1 qD.1.2:V cA.1.0.0:S iX.1.0:V "
+    "A.1.0.2 cA.1.0.1:S sA.1.0.0 A.0.1.0 cw.2.2.0:S cA.1.0.2:V sA.1.0.1 A.0.1.1 cw.2.2.1:S iY.0.0:V sA.1.0.2 "
+    "cA.0.1.0:S A.0.1.2 cA.0.1.1:S qX.0.0:V sA.0.1.0 A.0.1.3 cA.0.1.2:S sA.0.1.1 qX.1.0:V A.1.0.3 cA.0.1.3:S "
+    "sA.0.1.2 iY.1.0:V A.1.1.0 cA.1.0.3:S sA.0.1.3 A.1.1.1 qY.0.0:V cA.1.1.0:S sA.1.0.3 qY.1.0:V A.1.1.2 cA.1.1.1:S "
+    "sA.1.1.0 qW.2.0:V A.1.1.3 cA.1.1.2:S sA.1.1.1 qW.2.1:V B.0.0 cA.1.1.3:S qW.2.2:V sA.1.1.2 B.1.0 cB.0.0:S "
+    "iY.0.1:V B.2.0 sA.1.1.3 cB.1.0:S A.2.0.0 sB.0.0 cB.2.0:S iY.1.1:V A.2.0.1 sB.1.0 cA.2.0.0:S sB.2.0 A.2.0.2 "
+    "cA.2.0.1:S qY.0.1:V sA.2.0.0 A.2.0.3 qY.1.1:V cA.2.0.2:S sA.2.0.1 A.2.1.0 iY.0.2:V cA.2.0.3:S sA.2.0.2 B.0.1 "
+    "cA.2.1.0:S sA.2.0.3 B.1.1 iY.1.2:V cB.0.1:S A.2.1.1 sA.2.1.0 cB.1.1:S qY.0.2:V sB.0.1 A.2.1.2 cA.2.1.1:S "
+    "sB.1.1 qY.1.2:V B.2.1 cA.2.1.2:S sA.2.1.1 iX.0.1:V A.2.1.3 cB.2.1:S sA.2.1.2 B.0.2 cA.2.1.3:S iX.1.1:V sB.2.1 "
+    "B.1.2 cB.0.2:S B.2.2 sA.2.1.3 cB.1.2:S B.3.0 qX.0.1:V sB.0.2 B.3.1 cB.2.2:S qX.1.1:V sB.1.2 B.3.2 cB.3.0:S "
+    "iX.0.2:V sB.2.2 B.4.0 cB.3.1:S sB.3.0 B.4.1 cB.3.2:S cB.4.0:V B.4.2 sB.3.1 cB.4.1:S B.5.0 iX.1.2:V sB.3.2 "
+    "cB.4.2:S B.5.1 sB.4.0 B.5.2 cB.5.0:S sB.4.1 qX.0.2:V B.6.0 cB.5.1:S sB.4.2 cB.5.2:V B.6.1 sB.5.0 cB.6.0:S "
+    "qX.1.2:V B.6.2 sB.5.1 cB.6.1:S B.7.0 sB.5.2 cB.6.2:V B.7.1 sB.6.0 cB.7.0:S B.7.2 sB.6.1 cB.7.1:V B.8.0 sB.6.2 "
+    "cB.7.2:S B.8.1 sB.7.0 cB.8.0:V B.8.2 sB.7.1 cB.8.1:S B.9.0 cB.8.2:V sB.7.2 B.9.1 cB.9.0:S sB.8.0 B.9.2 "
+    "cB.9.1:V sB.8.1 B.10.0 cB.9.2:S sB.8.2 B.10.1 cB.10.0:V sB.9.0 B.10.2 cB.10.1:S sB.9.1 B.11.0 cB.10.2:V sB.9.2 "
+    "B.11.1 cB.11.0:S sB.10.0 B.11.2 cB.11.1:V sB.10.1 cB.11.2:S sB.10.2 sB.11.0 sB.11.1 sB.11.2"
 )
 
 
@@ -69,7 +70,7 @@ def tile_mla_pa_v_kernel(tc, x, w, freqs, grad_out, out_0, out_1):
             nc.sync.dma_start(out=ang[32 * r : 32 * r + 32, :, :].rearrange("p j f -> p (j f)"), in_=f_v)
 
         g_t = [keep.tile([P, 4, 1536], BF16, name="g%d" % h) for h in range(2)]
-        x_t = [keep.tile([P, 4, 1536], BF16, name="x%d" % h) for h in range(2)]
+        x_t = {}
         w_t = {}
         for name in LOADS.split(" "):
             if name[0] == "G":
@@ -77,11 +78,14 @@ def tile_mla_pa_v_kernel(tc, x, w, freqs, grad_out, out_0, out_1):
                 nc.sync.dma_start(out=g_t[h][:, j, :], in_=g_v[h, :, j, :])
             elif name[0] == "W":
                 n, jp = int(name[1]), int(name[2])
-                t = stage.tile([P, 2, 1536], BF16, name="w_raw", bufs=3)
-                nc.sync.dma_start(out=t[:], in_=w_v[n, :, 2 * jp : 2 * jp + 2, :])
-                w_t[n, jp] = t
+                if jp == 0:
+                    raw = stage.tile([P, 4, 1536], BF16, name="raw", bufs=4)
+                    w_t[n] = raw
+                nc.sync.dma_start(out=w_t[n][:, 2 * jp : 2 * jp + 2, :], in_=w_v[n, :, 2 * jp : 2 * jp + 2, :])
             else:
                 h = int(name[1])
+                raw = stage.tile([P, 4, 1536], BF16, name="raw", bufs=4)
+                x_t[h] = raw
                 nc.sync.dma_start(out=x_t[h][:], in_=x_v[h])
 
         ident = keep.tile([P, P], F32, name="ident")
@@ -118,7 +122,7 @@ def tile_mla_pa_v_kernel(tc, x, w, freqs, grad_out, out_0, out_1):
             return live[key]
 
         def grp():
-            t = stage.tile([P, 512, 4], BF16, name="grp", bufs=5, align_bytes=64)
+            t = stage.tile([P, 512, 4], BF16, name="grp", bufs=6, align_bytes=64)
             return t
 
         def dgn():
@@ -129,12 +133,8 @@ def tile_mla_pa_v_kernel(tc, x, w, freqs, grad_out, out_0, out_1):
             t = psum.tile([P, 512], F32, name="bank")
             return t
 
-        def res0():
-            t = stage.tile([P, 512], F32, name="res_0", bufs=4)
-            return t
-
-        def res1():
-            t = stage.tile([P, 1536], F32, name="res_1", bufs=5)
+        def res():
+            t = stage.tile([P, 512], F32, name="res", bufs=14)
             return t
 
         def srtd():
@@ -241,11 +241,11 @@ def tile_mla_pa_v_kernel(tc, x, w, freqs, grad_out, out_0, out_1):
             copy_out(eng, o, i)
 
         def t_tw(n, q, jp):
-            ww = w_t[n, jp][:].rearrange("p j c -> p (j c)").bitcast(F32).rearrange("p (j c) -> p j c", j=2)
+            ww = w_t[n][:].rearrange("p j c -> p (j c)").bitcast(F32).rearrange("p (j c) -> p j c", j=4)
             bv = get(("tw", n, q, jp), bank)[:].rearrange("p (j u r) -> p j u r", j=2, u=2)
             for i in range(2):
                 for u in range(2):
-                    nc.tensor.transpose(bv[:, i, u, :], ww[:, i, 256 * q + u : 256 * q + 256 : 2], ident[:])
+                    nc.tensor.transpose(bv[:, i, u, :], ww[:, 2 * jp + i, 256 * q + u : 256 * q + 256 : 2], ident[:])
 
         def t_cw(eng, n, q, jp):
             o, i = halves(get(("wg", n, q), grp)[:], jp, get(("tw", n, q, jp), bank))
@@ -269,11 +269,10 @@ def tile_mla_pa_v_kernel(tc, x, w, freqs, grad_out, out_0, out_1):
                 )
 
         def t_ca(eng, n, h, j):
-            res = get(("ra0", n, h, j), res0)
-            copy_out(eng, res[:].rearrange("p (r j) -> p r j", j=4), get(("a", n, h, j), bank)[:].rearrange("p (j r) -> p r j", j=4))
+            copy_out(eng, get(("ra0", n, h, j), res)[:].rearrange("p (r j) -> p r j", j=4), get(("a", n, h, j), bank)[:].rearrange("p (j r) -> p r j", j=4))
 
         def t_sa(n, h, j):
-            nc.sync.dma_start(out=o0_v[h, :, j, n * 512 : n * 512 + 512], in_=get(("ra0", n, h, j), res0)[:])
+            nc.sync.dma_start(out=o0_v[h, :, j, n * 512 : n * 512 + 512], in_=get(("ra0", n, h, j), res)[:])
 
         def t_ix(eng, h, c):
             copy_out(eng, get(("xg", h, c), grp)[:].rearrange("p (c i) t -> p c t i", i=4),
@@ -311,11 +310,10 @@ def tile_mla_pa_v_kernel(tc, x, w, freqs, grad_out, out_0, out_1):
                 )
 
         def t_cb(eng, m, n):
-            copy_out(eng, get(("rb1", m), res1)[:, n * 512 : n * 512 + 512], get(("b", m, n), bank)[:])
+            copy_out(eng, get(("rb1", m, n), res)[:], get(("b", m, n), bank)[:])
 
-        def t_sb(m, n=None):
-            cs = slice(0, 1536) if n is None else slice(n * 512, n * 512 + 512)
-            nc.sync.dma_start(out=out_1[m * 128 : m * 128 + 128, cs], in_=get(("rb1", m), res1)[:, cs])
+        def t_sb(m, n):
+            nc.sync.dma_start(out=out_1[m * 128 : m * 128 + 128, n * 512 : n * 512 + 512], in_=get(("rb1", m, n), res)[:])
 
         fns = {"warm": t_warm, "carg": t_carg, "cos": t_cos, "sort": t_sort, "tn": t_tn, "cn": t_cn, "qD": t_qd, "rA": t_ra, "rB": t_rb, "rC": t_rc, "tr": t_tr, "cr": t_cr,
                "tw": t_tw, "cw": t_cw, "qW": t_qw, "A": t_a, "cA": t_ca, "sA": t_sa, "iX": t_ix, "qX": t_qx, "iY": t_iy,

import math
from contextlib import ExitStack

import concourse.mybir as mybir
from concourse.masks import make_identity

F32 = mybir.dt.float32
BF16 = mybir.dt.bfloat16
U32 = mybir.dt.uint32
U8 = mybir.dt.uint8
E4M3 = mybir.dt.float8_e4m3fn_x4
E5M2 = mybir.dt.float8_e5m2_x4
ALU = mybir.AluOpType
ACT = mybir.ActivationFunctionType

P = 128
DIM = 1536
TOK = 1024
J = 1536
FLOPS = 2 * 2 * TOK * DIM * J

LOADS = (
    "G00 G01 G02 G03 W00 W01 W10 W11 W20 W21 G10 G11 G12 G13 X0 X1"
)
ORDER = (
    "warm.5 sort.0.0:V carg cos rA.0.0:V tn.0.0 warm.1 tn.0.1 warm.1 cn.0.0:S rA.0.1:V sort.0.1:S rB.0.0:V tw.0.0.0 "
    "warm.1 cn.0.1:S tw.0.1.0 warm.1 rB.0.1:V cw.0.0.0:S tw.0.2.0 warm.1 cw.0.1.0:S tw.0.0.1 warm.1 rC.0.0:V "
    "cw.0.2.0:S tw.0.1.1 warm.1 cw.0.0.1:S tw.0.2.1 warm.1 rC.0.1:V cw.0.1.1:S tn.0.2 warm.1 cw.0.2.1:S tn.0.3 "
    "warm.1 qW.0.0:V tr.0.0 warm.1 cn.0.2:S cn.0.3:V tr.0.1 warm.1 cr.0.0:S qW.0.1:V tw.1.0.0 warm.1 cr.0.1:S "
    "qD.0.0:V tw.1.0.1 warm.1 cw.1.0.0:S tw.1.1.0 warm.1 cw.1.0.1:S qD.0.2:V tw.1.1.1 warm.1 cw.1.1.0:S qW.0.2:V "
    "tw.1.2.0 warm.1 cw.1.1.1:S qW.1.0:V tw.1.2.1 warm.1 cw.1.2.0:S rA.1.0:V A.0.0.0 sort.1.0:S rB.1.0:V A.0.0.1 "
    "cA.0.0.0:S A.0.0.2 rA.1.1:V sort.1.1:S A.0.0.3 cA.0.0.1:V cA.0.0.2:S tn.1.0 rB.1.1:V tn.1.1 cA.0.0.3:S tn.1.2 "
    "cn.1.0:S tn.1.3 tw.2.0.0 rC.1.0:V cn.1.1:S tw.2.0.1 cn.1.2:S tw.2.1.0 rC.1.1:V tr.1.0 cn.1.3:S sA.0.0.0 "
    "tw.2.1.1 cw.1.2.1:S sA.0.0.1 qW.1.1:V tw.2.2.0 cr.1.0:S sA.0.0.2 qD.1.0:V tr.1.1 sA.0.0.3 cw.2.0.0:S tw.2.2.1 "
    "cr.1.1:S qW.1.2:V cw.2.0.1:S iX.0.0:V A.1.0.0 cw.2.1.0:S cw.2.1.1:S A.1.0.1 qD.1.2:V cA.1.0.0:S iX.1.0:V "
    "A.1.0.2 cA.1.0.1:S sA.1.0.0 A.0.1.0 cw.2.2.0:S cA.1.0.2:V sA.1.0.1 A.0.1.1 cw.2.2.1:S iY.0.0:V sA.1.0.2 "
    "cA.0.1.0:S A.0.1.2 cA.0.1.1:S qX.0.0:V sA.0.1.0 A.0.1.3 cA.0.1.2:S sA.0.1.1 qX.1.0:V A.1.0.3 cA.0.1.3:S "
    "sA.0.1.2 iY.1.0:V A.1.1.0 cA.1.0.3:S sA.0.1.3 A.1.1.1 qY.0.0:V cA.1.1.0:S sA.1.0.3 qY.1.0:V A.1.1.2 cA.1.1.1:S "
    "sA.1.1.0 qW.2.0:V A.1.1.3 cA.1.1.2:S sA.1.1.1 qW.2.1:V B.0.0 cA.1.1.3:S qW.2.2:V sA.1.1.2 B.1.0 cB.0.0:S "
    "iY.0.1:V B.2.0 sA.1.1.3 cB.1.0:S A.2.0.0 sB.0.0 cB.2.0:S iY.1.1:V A.2.0.1 sB.1.0 cA.2.0.0:S sB.2.0 A.2.0.2 "
    "cA.2.0.1:S qY.0.1:V sA.2.0.0 A.2.0.3 qY.1.1:V cA.2.0.2:S sA.2.0.1 A.2.1.0 iY.0.2:V cA.2.0.3:S sA.2.0.2 B.0.1 "
    "cA.2.1.0:S sA.2.0.3 B.1.1 iY.1.2:V cB.0.1:S A.2.1.1 sA.2.1.0 cB.1.1:S qY.0.2:V sB.0.1 A.2.1.2 cA.2.1.1:S "
    "sB.1.1 qY.1.2:V B.2.1 cA.2.1.2:S sA.2.1.1 iX.0.1:V A.2.1.3 cB.2.1:S sA.2.1.2 B.0.2 cA.2.1.3:S iX.1.1:V sB.2.1 "
    "B.1.2 cB.0.2:S B.2.2 sA.2.1.3 cB.1.2:S B.3.0 qX.0.1:V sB.0.2 B.3.1 cB.2.2:S qX.1.1:V sB.1.2 B.3.2 cB.3.0:S "
    "iX.0.2:V sB.2.2 B.4.0 cB.3.1:S sB.3.0 B.4.1 cB.3.2:S cB.4.0:V B.4.2 sB.3.1 cB.4.1:S B.5.0 iX.1.2:V sB.3.2 "
    "cB.4.2:S B.5.1 sB.4.0 B.5.2 cB.5.0:S sB.4.1 qX.0.2:V B.6.0 cB.5.1:S sB.4.2 cB.5.2:V B.6.1 sB.5.0 cB.6.0:S "
    "qX.1.2:V B.6.2 sB.5.1 cB.6.1:S B.7.0 sB.5.2 cB.6.2:V B.7.1 sB.6.0 cB.7.0:S B.7.2 sB.6.1 cB.7.1:V B.8.0 sB.6.2 "
    "cB.7.2:S B.8.1 sB.7.0 cB.8.0:V B.8.2 sB.7.1 cB.8.1:S B.9.0 cB.8.2:V sB.7.2 B.9.1 cB.9.0:S sB.8.0 B.9.2 "
    "cB.9.1:V sB.8.1 B.10.0 cB.9.2:S sB.8.2 B.10.1 cB.10.0:V sB.9.0 B.10.2 cB.10.1:S sB.9.1 B.11.0 cB.10.2:V sB.9.2 "
    "B.11.1 cB.11.0:S sB.10.0 B.11.2 cB.11.1:V sB.10.1 cB.11.2:S sB.10.2 sB.11.0 sB.11.1 sB.11.2"
)


def tile_mla_pa_v_kernel(tc, x, w, freqs, grad_out, out_0, out_1):
    nc = tc.nc
    x_v = x.rearrange("(h b) s c -> h (b s) c", h=2).rearrange("h (p j) c -> h p j c", j=4)
    g_v = grad_out.rearrange("(h b) s n q -> h (b s) (n q)", h=2).rearrange("h (p j) c -> h p j c", j=4)
    w_v = w.rearrange("(n p j) c -> n p j c", n=3, j=4)
    o0_v = out_0.rearrange("(h b) s c -> h (b s) c", h=2).rearrange("h (p j) c -> h p j c", j=4)
    f_v = freqs.rearrange("(q j) f -> q (j f)", j=4)

    with ExitStack() as ctx:
        keep = ctx.enter_context(tc.tile_pool(name="keep", bufs=1))
        stage = ctx.enter_context(tc.tile_pool(name="stage", bufs=2))
        psum = ctx.enter_context(tc.psum_pool(name="psum", bufs=8))
        ctx.enter_context(tc.manual_schedule())

        ang = keep.tile([P, 4, 32], BF16, name="ang")
        for r in range(4):
            nc.sync.dma_start(out=ang[32 * r : 32 * r + 32, :, :].rearrange("p j f -> p (j f)"), in_=f_v)

        g_t = [keep.tile([P, 4, 1536], BF16, name="g%d" % h) for h in range(2)]
        x_t = {}
        w_t = {}
        for name in LOADS.split(" "):
            if name[0] == "G":
                h, j = int(name[1]), int(name[2])
                nc.sync.dma_start(out=g_t[h][:, j, :], in_=g_v[h, :, j, :])
            elif name[0] == "W":
                n, jp = int(name[1]), int(name[2])
                if jp == 0:
                    raw = stage.tile([P, 4, 1536], BF16, name="raw", bufs=4)
                    w_t[n] = raw
                nc.sync.dma_start(out=w_t[n][:, 2 * jp : 2 * jp + 2, :], in_=w_v[n, :, 2 * jp : 2 * jp + 2, :])
            else:
                h = int(name[1])
                raw = stage.tile([P, 4, 1536], BF16, name="raw", bufs=4)
                x_t[h] = raw
                nc.sync.dma_start(out=x_t[h][:], in_=x_v[h])

        ident = keep.tile([P, P], F32, name="ident")

        absa = keep.tile([P, 128], F32, name="absa")
        carg = keep.tile([P, 128], F32, name="carg")
        cos2 = keep.tile([P, 4, 32, 2], F32, name="cos2")
        sin2 = keep.tile([P, 4, 32, 2], F32, name="sin2")
        nc.scalar.activation(out=absa[:], in_=ang[:].rearrange("p j f -> p (j f)"), func=ACT.Abs)
        nc.scalar.activation(out=sin2[:, :, :, 0], in_=ang[:], func=ACT.Sin)
        nc.scalar.activation(out=sin2[:, :, :, 1], in_=ang[:], func=ACT.Sin, scale=-1.0)

        def t_carg():
            nc.vector.tensor_scalar(out=carg[:], in0=absa[:], scalar1=-1.0, scalar2=math.pi / 2, op0=ALU.mult, op1=ALU.add)

        def t_cos():
            for e in range(2):
                nc.scalar.activation(out=cos2[:, :, :, e], in_=carg[:].rearrange("p (j f) -> p j f", j=4), func=ACT.Sin)

        dc = [keep.tile([P, 3, 512], U32, name="dc%d" % h, align_bytes=64) for h in range(2)]
        ds = [keep.tile([P, 3, 512], U8, name="ds%d" % h, align_bytes=64) for h in range(2)]
        wc = [keep.tile([P, 3, 512], U32, name="wc%d" % n, align_bytes=64) for n in range(3)]
        ws = [keep.tile([P, 3, 512], U8, name="ws%d" % n, align_bytes=64) for n in range(3)]
        xc = [keep.tile([P, 1536], U32, name="xc%d" % h, align_bytes=64) for h in range(2)]
        xs = [keep.tile([P, 1536], U8, name="xs%d" % h, align_bytes=64) for h in range(2)]
        yc = [keep.tile([P, 1536], U32, name="yc%d" % h, align_bytes=64) for h in range(2)]
        ys = [keep.tile([P, 1536], U8, name="ys%d" % h, align_bytes=64) for h in range(2)]
        rope = [keep.tile([P, 4, 512], BF16, name="rope%d" % h) for h in range(2)]
        live = {}

        def get(key, make):
            if key not in live:
                live[key] = make()
            return live[key]

        def grp():
            t = stage.tile([P, 512, 4], BF16, name="grp", bufs=6, align_bytes=64)
            return t

        def dgn():
            t = stage.tile([P, 2, 512, 4], BF16, name="dgn", bufs=1, align_bytes=64)
            return t

        def bank():
            t = psum.tile([P, 512], F32, name="bank")
            return t

        def res():
            t = stage.tile([P, 512], F32, name="res", bufs=14)
            return t

        def srtd():
            t = stage.tile([P, 2, 2, 2, 128], F32, name="sorted", bufs=2)
            return t

        def rota():
            t = stage.tile([P, 2, 8, 64], F32, name="rot_a", bufs=2)
            return t

        def rotb():
            t = stage.tile([P, 2, 8, 64], F32, name="rot_b", bufs=2)
            return t

        def words(t):
            return t.rearrange("p c t -> p (c t)").bitcast(F32).rearrange("p (c u) -> p c u", u=2)

        warm_in = keep.tile([P, 512], BF16, name="warm_in")
        nc.gpsimd.memset(warm_in[:], 0.0)
        make_identity(nc, ident[:])

        def t_warm(k):
            b = get("warm", bank)
            for i in range(k):
                nc.tensor.matmul(b[:], warm_in[:, 0:128], warm_in[:], start=True, stop=True)

        def copy_out(eng, out, in_):
            if eng == "S":
                nc.scalar.copy(out=out, in_=in_)
            else:
                nc.vector.tensor_copy(out=out, in_=in_)

        def quant(codes, fmt, scales, in_):
            nc.vector.quantize_mx(out=codes.bitcast(fmt), scales=scales, in_=in_.rearrange("p c t -> p (c t)"))

        def t_sort(eng, h, jj):
            srt = get(("sort", h, jj), srtd)
            gw = g_t[h][:, 2 * jj : 2 * jj + 2, :].rearrange("p j c -> p (j c)").bitcast(F32)
            gw = gw.rearrange("p (a n q) -> p a n q", a=4, n=4)[:, :, :, 0:64]
            so = srt[:].rearrange("p j q u (n i) -> p (j q) u n i", n=4)
            if eng == "V":
                copy_out(eng, so, gw.rearrange("p a n (i u) -> p a u n i", u=2))
            else:
                for u in range(2):
                    copy_out(eng, so[:, :, u], gw[:, :, :, u::2])

        def t_tn(h, j):
            srt = get(("sort", h, j // 2), srtd)
            b = get(("tn", h, j), bank)
            bv = b[:].rearrange("p (q u r) -> p q u r", q=2, u=2)
            for q in range(2):
                for u in range(2):
                    nc.tensor.transpose(bv[:, q, u, :], srt[:, j % 2, q, u, :], ident[:])

        def t_cn(eng, h, j):
            dg = get(("dgn", h), dgn)
            dgw = dg[:].rearrange("p q c t -> p (q c t)").bitcast(F32).rearrange("p (q c u) -> p q c u", q=2, u=2)
            bv = get(("tn", h, j), bank)[:].rearrange("p (q u r) -> p q u r", q=2, u=2)
            copy_out(eng, dgw[:, :, j * 128 : j * 128 + 128, :], bv.rearrange("p q u r -> p q r u"))

        def t_qd(h, q):
            if q == 0:
                quant(dc[h][:, 0:2, :].rearrange("p q c -> p (q c)"), E5M2, ds[h][:, 0:2, :].rearrange("p q c -> p (q c)"),
                      get(("dgn", h), dgn)[:].rearrange("p q c t -> p (q c) t"))
            else:
                quant(dc[h][:, 2, :], E5M2, ds[h][:, 2, :], get(("dr", h), grp)[:])

        def rope_of(h, js):
            return g_t[h][:, js, :].rearrange("p j (n q) -> p j n q", q=192)[:, :, :, 128:]

        def t_ra(h, jj):
            js = slice(2 * jj, 2 * jj + 2)
            c2 = cos2[:, js].rearrange("p j f e -> p j (f e)").unsqueeze(2).to_broadcast([P, 2, 8, 64])
            nc.vector.tensor_tensor(out=get(("ra", h, jj), rota)[:], in0=rope_of(h, js), in1=c2, op=ALU.mult)

        def t_rb(h, jj):
            gr = rope_of(h, slice(2 * jj, 2 * jj + 2))
            b = get(("rb", h, jj), rotb)
            swapped = gr.rearrange("p j n (f e) -> p j n f e", e=2)[:, :, :, :, ::-1]
            s2 = sin2[:, 2 * jj : 2 * jj + 2].unsqueeze(2).to_broadcast([P, 2, 8, 32, 2])
            nc.vector.tensor_tensor(out=b[:].rearrange("p j n (f e) -> p j n f e", e=2), in0=swapped, in1=s2, op=ALU.mult)

        def t_rc(h, jj):
            nc.vector.tensor_tensor(
                out=rope[h][:, 2 * jj : 2 * jj + 2, :],
                in0=get(("ra", h, jj), rota)[:].rearrange("p j n q -> p j (n q)"),
                in1=get(("rb", h, jj), rotb)[:].rearrange("p j n q -> p j (n q)"),
                op=ALU.add,
            )

        def t_tr(h, jj):
            bv = get(("tr", h, jj), bank)[:].rearrange("p (j u r) -> p j u r", j=2, u=2)
            rw = rope[h][:].rearrange("p j c -> p (j c)").bitcast(F32).rearrange("p (j c) -> p j c", j=4)
            for i in range(2):
                for u in range(2):
                    nc.tensor.transpose(bv[:, i, u, :], rw[:, 2 * jj + i, u::2], ident[:])

        def halves(dst, jp, b):
            out = words(dst)[:, jp * 256 : jp * 256 + 256, :].rearrange("p (j r) u -> p j r u", j=2)
            return out, b[:].rearrange("p (j u r) -> p j r u", j=2, u=2)

        def t_cr(eng, h, jj):
            o, i = halves(get(("dr", h), grp)[:], jj, get(("tr", h, jj), bank))
            copy_out(eng, o, i)

        def t_tw(n, q, jp):
            ww = w_t[n][:].rearrange("p j c -> p (j c)").bitcast(F32).rearrange("p (j c) -> p j c", j=4)
            bv = get(("tw", n, q, jp), bank)[:].rearrange("p (j u r) -> p j u r", j=2, u=2)
            for i in range(2):
                for u in range(2):
                    nc.tensor.transpose(bv[:, i, u, :], ww[:, 2 * jp + i, 256 * q + u : 256 * q + 256 : 2], ident[:])

        def t_cw(eng, n, q, jp):
            o, i = halves(get(("wg", n, q), grp)[:], jp, get(("tw", n, q, jp), bank))
            copy_out(eng, o, i)

        def t_qw(n, q):
            quant(wc[n][:, q, :], E4M3, ws[n][:, q, :], get(("wg", n, q), grp)[:])

        def t_a(n, h, j):
            acc = get(("a", n, h, j), bank)
            cols = slice(j * 128, j * 128 + 128)
            for q in range(3):
                nc.tensor.matmul_mx(
                    out=acc[:],
                    lhsT=dc[h][:, q, cols].bitcast(E5M2),
                    lhsT_scale=ds[h][:, q, cols],
                    rhs=wc[n][:, q, :].bitcast(E4M3),
                    rhs_scale=ws[n][:, q, :],
                    start=(q == 0),
                    stop=(q == 2),
                )

        def t_ca(eng, n, h, j):
            copy_out(eng, get(("ra0", n, h, j), res)[:].rearrange("p (r j) -> p r j", j=4), get(("a", n, h, j), bank)[:].rearrange("p (j r) -> p r j", j=4))

        def t_sa(n, h, j):
            nc.sync.dma_start(out=o0_v[h, :, j, n * 512 : n * 512 + 512], in_=get(("ra0", n, h, j), res)[:])

        def t_ix(eng, h, c):
            copy_out(eng, get(("xg", h, c), grp)[:].rearrange("p (c i) t -> p c t i", i=4),
                     x_t[h][:, :, c * 512 : c * 512 + 512].rearrange("p t (c i) -> p c t i", i=4))

        def t_qx(h, c):
            cs = slice(c * 512, c * 512 + 512)
            quant(xc[h][:, cs], E4M3, xs[h][:, cs], get(("xg", h, c), grp)[:])

        def t_iy(eng, h, c):
            yg = get(("yg", h, c), grp)
            if c < 2:
                src = g_t[h][:, :, c * 768 : c * 768 + 768].rearrange("p t (n q) -> p t n q", n=4)[:, :, :, 0:128]
                copy_out(eng, yg[:].rearrange("p (n k) t -> p n k t", n=4), src.rearrange("p t n k -> p n k t"))
            else:
                copy_out(eng, yg[:].rearrange("p (c i) t -> p c t i", i=4), rope[h][:].rearrange("p t (c i) -> p c t i", i=4))

        def t_qy(h, c):
            cs = slice(c * 512, c * 512 + 512)
            quant(yc[h][:, cs], E5M2, ys[h][:, cs], get(("yg", h, c), grp)[:])

        def t_b(m, n):
            acc = get(("b", m, n), bank)
            cols = slice(m * 128, m * 128 + 128)
            ns = slice(n * 512, n * 512 + 512)
            for h in range(2):
                nc.tensor.matmul_mx(
                    out=acc[:],
                    lhsT=xc[h][:, cols].bitcast(E4M3),
                    lhsT_scale=xs[h][:, cols],
                    rhs=yc[h][:, ns].bitcast(E5M2),
                    rhs_scale=ys[h][:, ns],
                    start=(h == 0),
                    stop=(h == 1),
                )

        def t_cb(eng, m, n):
            copy_out(eng, get(("rb1", m, n), res)[:], get(("b", m, n), bank)[:])

        def t_sb(m, n):
            nc.sync.dma_start(out=out_1[m * 128 : m * 128 + 128, n * 512 : n * 512 + 512], in_=get(("rb1", m, n), res)[:])

        fns = {"warm": t_warm, "carg": t_carg, "cos": t_cos, "sort": t_sort, "tn": t_tn, "cn": t_cn, "qD": t_qd, "rA": t_ra, "rB": t_rb, "rC": t_rc, "tr": t_tr, "cr": t_cr,
               "tw": t_tw, "cw": t_cw, "qW": t_qw, "A": t_a, "cA": t_ca, "sA": t_sa, "iX": t_ix, "qX": t_qx, "iY": t_iy,
               "qY": t_qy, "B": t_b, "cB": t_cb, "sB": t_sb}
        for tok in ORDER.split(" "):
            parts = tok.split(":")
            f = parts[0].split(".")
            args = [int(a) for a in f[1:]]
            if len(parts) == 2 and f[0] in ("sort", "cn", "cr", "cw", "cA", "iX", "iY", "cB"):
                fns[f[0]](parts[1], *args)
            else:
                fns[f[0]](*args)
